import numpy as np
import ml_dtypes


def mxq(x, axis, fmt="e4m3"):
    dtype, down = {"e4m3": (ml_dtypes.float8_e4m3fn, 7), "e5m2": (ml_dtypes.float8_e5m2, 14)}[fmt]
    v = np.moveaxis(np.asarray(x, np.float32).astype(ml_dtypes.bfloat16).astype(np.float64), axis, -1)
    blocks = v.reshape(v.shape[:-1] + (-1, 32))
    amax = np.abs(blocks).max(-1, keepdims=True)
    byte = np.maximum(np.where(amax > 0, np.frexp(amax)[1] - 1 + 127, 0) - down, 1)
    scale = np.exp2(byte - 127.0)
    codes = (blocks / scale).astype(np.float32).astype(dtype).astype(np.float64)
    return np.moveaxis((codes * scale).reshape(v.shape), -1, axis)


WIDE = False


def mx_kscale(k):
    if not WIDE:
        return np.ones(k)
    levels = np.array([10, -10, 5, -5, 0])
    if k % 512:
        return np.exp2(np.random.permutation(np.resize(levels, k // 32))).repeat(32)
    a = np.empty((k // 512, 16))
    for p in range(k // 512):
        a[p, :8] = np.random.permutation(np.resize(levels, 8))
        for g in range(8):
            far = levels[np.abs(levels - a[p, g]) >= 10]
            a[p, g + 8] = far[np.random.randint(len(far))]
    return np.exp2(a.ravel()).repeat(32)


BF16 = ml_dtypes.bfloat16


def bf(x):
    return np.asarray(x, np.float32).astype(BF16)


def f64(x):
    return np.asarray(x).astype(np.float64)


B, I, H = 8192, 512, 128
MXK = 16 * 32


def sigmoid(v):
    return 1.0 / (1.0 + np.exp(-v))


def lin(a, w):
    if a.shape[1] % MXK == 0:
        return mxq(a, 1, "e4m3") @ mxq(w, 1, "e4m3").T
    return a @ w.T


def setup_inputs():
    s = mx_kscale(I)
    t = mx_kscale(H) if H % MXK == 0 else np.ones(H)
    inp = {"incoming": bf(np.random.standard_normal((B, I)) * s),
           "old_h": bf(np.random.standard_normal((B, H)) * t),
           "old_c": bf(np.random.standard_normal((B, H)))}
    for n in ("i", "o", "f", "c"):
        inp["w_" + n] = bf(np.random.standard_normal((H, I)) / np.sqrt(I) / s)
        inp["b_" + n] = bf(np.random.standard_normal(H) * 0.5)
        inp["u_" + n] = bf(np.random.standard_normal((H, H)) / np.sqrt(H) / t)
    return inp


def reference(incoming, old_h, old_c, w_i, b_i, u_i, w_o, b_o, u_o, w_f, b_f, u_f, w_c, b_c, u_c):
    W = np.concatenate([f64(w_i), f64(w_o), f64(w_f), f64(w_c)], axis=0)
    U = np.concatenate([f64(u_i), f64(u_o), f64(u_f), f64(u_c)], axis=0)
    b = np.concatenate([f64(b_i), f64(b_o), f64(b_f), f64(b_c)], axis=0)
    gates = lin(f64(incoming), W) + lin(f64(old_h), U) + b
    gi, go, gf, gc = np.split(gates, 4, axis=-1)
    i = sigmoid(gi)
    o = sigmoid(go)
    f = sigmoid(gf)
    c_tilde = np.tanh(gc)
    new_c = f * f64(old_c) + i * c_tilde
    new_h = o * np.tanh(new_c)
    return (new_h, new_c)

@@ -1,0 +1,320 @@
+from contextlib import ExitStack
+
+import concourse.mybir as mybir
+from concourse.masks import make_identity
+
+F32 = mybir.dt.float32
+BF16 = mybir.dt.bfloat16
+U32 = mybir.dt.uint32
+U8 = mybir.dt.uint8
+FP8X4 = mybir.dt.float8_e4m3fn_x4
+ACT = mybir.ActivationFunctionType
+ALU = mybir.AluOpType
+
+P = 128
+BATCH = 8192
+IN_F = 512
+HID = 128
+NT = BATCH // P
+GT = 4
+NG = NT // GT
+GW = GT * P
+HC_SIZES = [2, 2, 4, 4, 4]
+
+FLOPS = 2 * BATCH * (IN_F + HID) * 4 * HID
+
+
+def tile_lstmcell_t_kernel(
+    tc, incoming, old_h, old_c, w_i, b_i, u_i, w_o, b_o, u_o, w_f, b_f, u_f, w_c, b_c, u_c, out_0, out_1
+):
+    nc = tc.nc
+    gate_w = [w_i, w_f, w_o, w_c]
+    gate_u = [u_i, u_f, u_o, u_c]
+    gate_b = [b_i, b_f, b_o, b_c]
+
+    x_rows = incoming.rearrange("(p t) k -> p (t k)", t=NT)
+    h_rows = old_h.rearrange("(p t) k -> p (t k)", t=NT)
+    c_rows = old_c.rearrange("(p t) k -> p (t k)", t=NT)
+    nh_rows = out_0.rearrange("(p t) k -> p (t k)", t=NT)
+    cell_rows = out_1.rearrange("(p t) k -> p (t k)", t=NT)
+
+    with ExitStack() as ctx:
+        const = ctx.enter_context(tc.tile_pool(name="const", bufs=1))
+        resident = ctx.enter_context(tc.tile_pool(name="resident", bufs=1))
+        work2 = ctx.enter_context(tc.tile_pool(name="work2", bufs=2))
+        work3 = ctx.enter_context(tc.tile_pool(name="work3", bufs=3))
+        work4 = ctx.enter_context(tc.tile_pool(name="work4", bufs=4))
+        psum = ctx.enter_context(tc.psum_pool(name="psum", bufs=8))
+        ctx.enter_context(tc.manual_schedule())
+
+        ident_f = const.tile([P, P], F32, name="ident_f")
+        make_identity(nc, ident_f[:])
+        ident_b = const.tile([P, P], BF16, name="ident_b")
+        make_identity(nc, ident_b[:])
+
+        warm = const.tile([P, 1], F32, name="warm")
+        nc.vector.memset(warm[:], 0.0)
+        warm_out = const.tile([P, 1], F32, name="warm_out")
+        nc.scalar.activation(out=warm_out[:], in_=warm[:], func=ACT.Sigmoid)
+
+        x_sb = {}
+        h_of = {}
+        c_of = {}
+
+        def load_x(j):
+            x_sb[j] = resident.tile([P, GT * IN_F], BF16, name="x%d" % j)
+            nc.sync.dma_start(out=x_sb[j][:], in_=x_rows[:, j * GT * IN_F : (j + 1) * GT * IN_F])
+
+        def load_hc(m, rows, table, letter):
+            first = sum(HC_SIZES[:m])
+            t = resident.tile([P, HC_SIZES[m] * GW], BF16, name="%s%d" % (letter, m))
+            nc.sync.dma_start(out=t[:], in_=rows[:, first * GW : (first + HC_SIZES[m]) * GW])
+            for r in range(HC_SIZES[m]):
+                table[first + r] = t[:, r * GW : (r + 1) * GW]
+
+        def load_h(m):
+            load_hc(m, h_rows, h_of, "h")
+
+        def load_c(m):
+            load_hc(m, c_rows, c_of, "c")
+
+        w_sb = const.tile([P, 4 * IN_F], BF16, name="w_sb")
+        for n in range(4):
+            nc.sync.dma_start(out=w_sb[:, n * IN_F : (n + 1) * IN_F], in_=gate_w[n])
+        load_x(0)
+        load_h(0)
+        u_sb = const.tile([P, 4 * HID], BF16, name="u_sb")
+        for n in range(4):
+            nc.scalar.dma_start(out=u_sb[:, n * HID : (n + 1) * HID], in_=gate_u[n])
+        b_rows = const.tile([P, P], BF16, name="b_rows")
+        nc.vector.memset(b_rows[:], 0.0)
+        for n in range(4):
+            nc.scalar.dma_start(out=b_rows[n : n + 1, :], in_=gate_b[n].rearrange("(o h) -> o h", o=1))
+        load_x(1)
+        load_x(2)
+        load_c(0)
+        load_h(1)
+        load_x(3)
+        load_c(1)
+        load_x(4)
+        load_h(2)
+        load_x(5)
+        load_c(2)
+        load_x(6)
+        load_x(7)
+        load_x(8)
+        load_h(3)
+        load_c(3)
+        load_x(9)
+        load_x(10)
+        load_x(11)
+        load_x(12)
+        load_h(4)
+        load_c(4)
+        load_x(13)
+        load_x(14)
+        load_x(15)
+
+        def transpose_words(src, grouped, copies):
+            words = src[:].bitcast(F32)
+            out_words = grouped[:].bitcast(F32).rearrange("q (s c u) -> q s c u", s=4, u=2)
+            for half in range(2):
+                bank = psum.tile([P, 512], F32, name="bank", tag="bank")
+                for s in range(2):
+                    for u in range(2):
+                        first = (2 * half + s) * 256
+                        nc.tensor.transpose(
+                            bank[:, (2 * s + u) * P : (2 * s + u + 1) * P],
+                            words[:, first + u : first + 256 : 2],
+                            ident_f[:],
+                        )
+                copies[half](
+                    out=out_words[:, 2 * half : 2 * half + 2],
+                    in_=bank[:].rearrange("q (s u c) -> q s c u", s=2, u=2),
+                )
+
+        grouped = {}
+        codes = {}
+        scales = {}
+        h_t_sb = {}
+        a_sb = {}
+        acts = {}
+        fc = {}
+        ic = {}
+        cell = {}
+        tanh_c = {}
+
+        def stage_tx(j, copies):
+            grouped[j] = work2.tile([P, GW * 4], BF16, name="grouped", align_bytes=64)
+            transpose_words(x_sb[j], grouped[j], copies)
+
+        def stage_th(j):
+            ht = psum.tile([P, GW], BF16, name="ht", tag="bank")
+            for s in range(GT):
+                nc.tensor.transpose(ht[:, s * P : (s + 1) * P], h_of[j][:, s * P : (s + 1) * P], ident_b[:])
+            h_t_sb[j] = work4.tile([P, GW], BF16, name="h_t_sb")
+            nc.vector.tensor_copy(out=h_t_sb[j][:], in_=ht[:])
+
+        def stage_q(j):
+            codes[j] = work3.tile([P, GW], U32, name="codes", align_bytes=64)
+            scales[j] = work3.tile([P, GW], U8, name="scales", align_bytes=64)
+            nc.vector.quantize_mx(out=codes[j][:].bitcast(FP8X4), scales=scales[j][:], in_=grouped[j][:])
+
+        def stage_mx(j, on_scalar):
+            a_sb[j] = work3.tile([P, 4 * GW], F32, name="a_sb")
+            for n in range(4):
+                mx = psum.tile([P, GW], F32, name="mx", tag="bank")
+                nc.tensor.matmul_mx(
+                    out=mx[:],
+                    lhsT=w_codes[:, n * P : (n + 1) * P].bitcast(FP8X4),
+                    lhsT_scale=w_scales[:, n * P : (n + 1) * P],
+                    rhs=codes[j][:].bitcast(FP8X4),
+                    rhs_scale=scales[j][:],
+                    start=True,
+                    stop=True,
+                )
+                if n in on_scalar:
+                    nc.scalar.activation(
+                        out=a_sb[j][:, n * GW : (n + 1) * GW], in_=mx[:], func=ACT.Identity, bias=bias_col[:, n : n + 1]
+                    )
+                else:
+                    nc.vector.tensor_scalar_add(
+                        out=a_sb[j][:, n * GW : (n + 1) * GW], in0=mx[:], scalar1=bias_col[:, n : n + 1]
+                    )
+
+        def stage_g(j, s0, s1):
+            if s0 == 0:
+                acts[j] = work3.tile([P, GT * 4 * HID], F32, name="acts")
+            for s in range(s0, s1):
+                g = psum.tile([P, 4 * HID], F32, name="g", tag="bank")
+                for n in range(4):
+                    nc.tensor.matmul(
+                        out=g[:, n * HID : (n + 1) * HID],
+                        lhsT=a_sb[j][:, n * GW + s * P : n * GW + (s + 1) * P],
+                        rhs=ident_f[:],
+                        is_transpose=True,
+                        start=(n == 0),
+                        stop=False,
+                    )
+                nc.tensor.matmul(
+                    out=g[:], lhsT=h_t_sb[j][:, s * P : (s + 1) * P], rhs=u_t[:], start=False, stop=True
+                )
+                base = s * 4 * HID
+                nc.scalar.activation(out=acts[j][:, base : base + 3 * HID], in_=g[:, 0 : 3 * HID], func=ACT.Sigmoid)
+                nc.scalar.activation(
+                    out=acts[j][:, base + 3 * HID : base + 4 * HID], in_=g[:, 3 * HID : 4 * HID], func=ACT.Tanh
+                )
+
+        def by_tile(ap, tiles):
+            return ap.rearrange("p (t h) -> p t h", t=tiles)
+
+        def gate(j, n, s0, s1):
+            return acts[j][:].rearrange("p (t n h) -> p t n h", t=GT, n=4)[:, s0:s1, n, :]
+
+        def stage_prod(j, eng, s0, s1):
+            tiles = s1 - s0
+            key = (j, s0)
+            fc[key] = work2.tile([P, tiles * HID], F32, name="fc")
+            ic[key] = work2.tile([P, tiles * HID], F32, name="ic")
+            eng.tensor_tensor(
+                out=by_tile(fc[key][:], tiles),
+                in0=gate(j, 1, s0, s1),
+                in1=by_tile(c_of[j][:, s0 * HID : s1 * HID], tiles),
+                op=ALU.mult,
+            )
+            eng.tensor_tensor(out=by_tile(ic[key][:], tiles), in0=gate(j, 0, s0, s1), in1=gate(j, 3, s0, s1), op=ALU.mult)
+
+        def stage_add(j, s0, s1):
+            key = (j, s0)
+            cell[key] = work4.tile([P, (s1 - s0) * HID], F32, name="cell")
+            nc.vector.tensor_tensor(out=cell[key][:], in0=fc[key][:], in1=ic[key][:], op=ALU.add)
+            nc.sync.dma_start(out=cell_rows[:, j * GW + s0 * HID : j * GW + s1 * HID], in_=cell[key][:])
+
+        def stage_tanh(j, s0, s1):
+            key = (j, s0)
+            tanh_c[key] = work2.tile([P, (s1 - s0) * HID], F32, name="tanh_c")
+            nc.scalar.activation(out=tanh_c[key][:], in_=cell[key][:], func=ACT.Tanh)
+
+        def stage_h(j, s0, s1):
+            tiles = s1 - s0
+            nh = work4.tile([P, tiles * HID], F32, name="nh")
+            nc.vector.tensor_tensor(
+                out=by_tile(nh[:], tiles), in0=gate(j, 2, s0, s1), in1=by_tile(tanh_c[(j, s0)][:], tiles), op=ALU.mult
+            )
+            nc.sync.dma_start(out=nh_rows[:, j * GW + s0 * HID : j * GW + s1 * HID], in_=nh[:])
+
+        on_s = [nc.scalar.copy, nc.scalar.copy]
+
+        w_grouped = const.tile([P, 4 * P * 4], BF16, name="w_grouped", align_bytes=64)
+        transpose_words(w_sb, w_grouped, [nc.vector.tensor_copy, nc.vector.tensor_copy])
+        w_codes = const.tile([P, 4 * P], U32, name="w_codes", align_bytes=64)
+        w_scales = const.tile([P, 4 * P], U8, name="w_scales", align_bytes=64)
+        nc.vector.quantize_mx(out=w_codes[:].bitcast(FP8X4), scales=w_scales[:], in_=w_grouped[:])
+
+        stage_tx(0, [nc.scalar.copy, nc.vector.tensor_copy])
+        stage_th(0)
+
+        ut = psum.tile([P, 4 * HID], BF16, name="ut", tag="bank")
+        for n in range(4):
+            nc.tensor.transpose(ut[:, n * HID : (n + 1) * HID], u_sb[:, n * HID : (n + 1) * HID], ident_b[:])
+        u_t = const.tile([P, 4 * HID], BF16, name="u_t")
+        nc.vector.tensor_copy(out=u_t[:], in_=ut[:])
+        bt = psum.tile([P, P], BF16, name="bt", tag="bank")
+        nc.tensor.transpose(bt[:], b_rows[:], ident_b[:])
+        bias_col = const.tile([P, 4], F32, name="bias_col")
+        nc.vector.tensor_copy(out=bias_col[:], in_=bt[:, 0:4])
+
+        stage_q(0)
+        stage_tx(1, on_s)
+        stage_th(1)
+        stage_mx(0, [1, 3])
+        stage_q(1)
+        stage_tx(2, on_s)
+        stage_th(2)
+        stage_mx(1, [])
+        stage_q(2)
+        for i in range(NG - 2):
+            if i + 3 < NG:
+                stage_tx(i + 3, on_s)
+                stage_th(i + 3)
+            if i >= 1:
+                stage_prod(i - 1, nc.gpsimd, 0, GT)
+            if i + 3 < NG:
+                stage_q(i + 3)
+            if i >= 1:
+                stage_add(i - 1, 0, GT)
+            if i >= 2:
+                stage_h(i - 2, 0, GT)
+            stage_g(i, 0, GT)
+            if i >= 1:
+                stage_tanh(i - 1, 0, GT)
+            if i + 2 < NG:
+                stage_mx(i + 2, [])
+
+        ga = NG - 3
+        gb = NG - 2
+        gc = NG - 1
+        stage_prod(ga, nc.gpsimd, 0, GT)
+        stage_g(gb, 0, 4)
+        stage_h(ga - 1, 0, GT)
+        stage_prod(gb, nc.vector, 0, 2)
+        stage_add(gb, 0, 2)
+        stage_add(ga, 0, GT)
+        stage_g(gc, 0, 2)
+        stage_tanh(ga, 0, GT)
+        stage_prod(gb, nc.vector, 2, 4)
+        stage_add(gb, 2, 4)
+        stage_tanh(gb, 0, 2)
+        stage_h(ga, 0, GT)
+        stage_g(gc, 2, 4)
+        stage_tanh(gb, 2, 4)
+        stage_h(gb, 0, 2)
+        stage_prod(gc, nc.vector, 0, 2)
+        stage_add(gc, 0, 2)
+        stage_h(gb, 2, 4)
+        stage_tanh(gc, 0, 2)
+        stage_prod(gc, nc.vector, 2, 4)
+        stage_add(gc, 2, 4)
+        stage_h(gc, 0, 2)
+        stage_tanh(gc, 2, 4)
+        stage_h(gc, 2, 4)

@@ -115,57 +115,74 @@ def tile_lstmcell_t_kernel(
         load_x(14)
         load_x(15)
 
-        def transpose_words(src, grouped, copies):
-            words = src[:].bitcast(F32)
-            out_words = grouped[:].bitcast(F32).rearrange("q (s c u) -> q s c u", s=4, u=2)
-            for half in range(2):
-                bank = psum.tile([P, 512], F32, name="bank", tag="bank")
-                for s in range(2):
-                    for u in range(2):
-                        first = (2 * half + s) * 256
-                        nc.tensor.transpose(
-                            bank[:, (2 * s + u) * P : (2 * s + u + 1) * P],
-                            words[:, first + u : first + 256 : 2],
-                            ident_f[:],
-                        )
-                copies[half](
-                    out=out_words[:, 2 * half : 2 * half + 2],
-                    in_=bank[:].rearrange("q (s u c) -> q s c u", s=2, u=2),
-                )
-
+        parted = {}
         grouped = {}
         codes = {}
         scales = {}
+        h_bank = {}
         h_t_sb = {}
         a_sb = {}
+        mx_bank = {}
         acts = {}
         fc = {}
         ic = {}
         cell = {}
         tanh_c = {}
+        on_scalar = nc.scalar.copy
+        on_vector = nc.vector.tensor_copy
+        on_gpsimd = nc.gpsimd.tensor_copy
 
-        def stage_tx(j, copies):
-            grouped[j] = work2.tile([P, GW * 4], BF16, name="grouped", align_bytes=64)
-            transpose_words(x_sb[j], grouped[j], copies)
+        def half_words(src, half):
+            return src[:].bitcast(F32)[:, half * 512 : (half + 1) * 512]
+
+        def stage_part(j, half, copy):
+            parted[(j, half)] = work3.tile([P, 512], F32, name="parted%d" % half)
+            copy(
+                out=parted[(j, half)][:].rearrange("q (u w) -> q u w", u=2),
+                in_=half_words(x_sb[j], half).rearrange("q (w u) -> q u w", u=2),
+            )
+
+        def transpose_half(src, dst, half, copy, part):
+            out_words = dst[:].bitcast(F32).rearrange("q (s c u) -> q s c u", s=4, u=2)
+            bank = psum.tile([P, 512], F32, name="bank", tag="bank")
+            for s in range(2):
+                for u in range(2):
+                    if part is None:
+                        ap = half_words(src, half)[:, s * 256 + u : (s + 1) * 256 : 2]
+                    else:
+                        ap = part[:, u * 256 + s * P : u * 256 + (s + 1) * P]
+                    nc.tensor.transpose(bank[:, (2 * s + u) * P : (2 * s + u + 1) * P], ap, ident_f[:])
+            copy(
+                out=out_words[:, 2 * half : 2 * half + 2],
+                in_=bank[:].rearrange("q (s u c) -> q s c u", s=2, u=2),
+            )
+
+        def stage_tx(j, half, copy):
+            if half == 0:
+                grouped[j] = work2.tile([P, GW * 4], BF16, name="grouped", align_bytes=64)
+            part = parted.get((j, half))
+            transpose_half(x_sb[j], grouped[j], half, copy, None if part is None else part[:])
 
         def stage_th(j):
-            ht = psum.tile([P, GW], BF16, name="ht", tag="bank")
+            h_bank[j] = psum.tile([P, GW], BF16, name="ht", tag="bank")
             for s in range(GT):
-                nc.tensor.transpose(ht[:, s * P : (s + 1) * P], h_of[j][:, s * P : (s + 1) * P], ident_b[:])
+                nc.tensor.transpose(h_bank[j][:, s * P : (s + 1) * P], h_of[j][:, s * P : (s + 1) * P], ident_b[:])
+
+        def stage_hcopy(j, copy):
             h_t_sb[j] = work4.tile([P, GW], BF16, name="h_t_sb")
-            nc.vector.tensor_copy(out=h_t_sb[j][:], in_=ht[:])
+            copy(out=h_t_sb[j][:], in_=h_bank[j][:])
 
         def stage_q(j):
             codes[j] = work3.tile([P, GW], U32, name="codes", align_bytes=64)
             scales[j] = work3.tile([P, GW], U8, name="scales", align_bytes=64)
             nc.vector.quantize_mx(out=codes[j][:].bitcast(FP8X4), scales=scales[j][:], in_=grouped[j][:])
 
-        def stage_mx(j, on_scalar):
+        def stage_mx(j):
             a_sb[j] = work3.tile([P, 4 * GW], F32, name="a_sb")
             for n in range(4):
-                mx = psum.tile([P, GW], F32, name="mx", tag="bank")
+                mx_bank[(j, n)] = psum.tile([P, GW], F32, name="mx", tag="bank")
                 nc.tensor.matmul_mx(
-                    out=mx[:],
+                    out=mx_bank[(j, n)][:],
                     lhsT=w_codes[:, n * P : (n + 1) * P].bitcast(FP8X4),
                     lhsT_scale=w_scales[:, n * P : (n + 1) * P],
                     rhs=codes[j][:].bitcast(FP8X4),
@@ -173,37 +190,42 @@ def tile_lstmcell_t_kernel(
                     start=True,
                     stop=True,
                 )
-                if n in on_scalar:
-                    nc.scalar.activation(
-                        out=a_sb[j][:, n * GW : (n + 1) * GW], in_=mx[:], func=ACT.Identity, bias=bias_col[:, n : n + 1]
-                    )
-                else:
-                    nc.vector.tensor_scalar_add(
-                        out=a_sb[j][:, n * GW : (n + 1) * GW], in0=mx[:], scalar1=bias_col[:, n : n + 1]
-                    )
 
-        def stage_g(j, s0, s1):
-            if s0 == 0:
-                acts[j] = work3.tile([P, GT * 4 * HID], F32, name="acts")
-            for s in range(s0, s1):
-                g = psum.tile([P, 4 * HID], F32, name="g", tag="bank")
-                for n in range(4):
-                    nc.tensor.matmul(
-                        out=g[:, n * HID : (n + 1) * HID],
-                        lhsT=a_sb[j][:, n * GW + s * P : n * GW + (s + 1) * P],
-                        rhs=ident_f[:],
-                        is_transpose=True,
-                        start=(n == 0),
-                        stop=False,
-                    )
-                nc.tensor.matmul(
-                    out=g[:], lhsT=h_t_sb[j][:, s * P : (s + 1) * P], rhs=u_t[:], start=False, stop=True
-                )
-                base = s * 4 * HID
-                nc.scalar.activation(out=acts[j][:, base : base + 3 * HID], in_=g[:, 0 : 3 * HID], func=ACT.Sigmoid)
+        def stage_mxcopy(j, n, scalar):
+            if scalar:
                 nc.scalar.activation(
-                    out=acts[j][:, base + 3 * HID : base + 4 * HID], in_=g[:, 3 * HID : 4 * HID], func=ACT.Tanh
+                    out=a_sb[j][:, n * GW : (n + 1) * GW], in_=mx_bank[(j, n)][:], func=ACT.Identity, bias=bias_col[:, n : n + 1]
                 )
+            elif n == 3:
+                nc.vector.tensor_scalar(
+                    out=a_sb[j][:, n * GW : (n + 1) * GW],
+                    in0=mx_bank[(j, n)][:],
+                    scalar1=bias_col[:, n : n + 1],
+                    scalar2=2.0,
+                    op0=ALU.add,
+                    op1=ALU.mult,
+                )
+            else:
+                nc.vector.tensor_scalar_add(
+                    out=a_sb[j][:, n * GW : (n + 1) * GW], in0=mx_bank[(j, n)][:], scalar1=bias_col[:, n : n + 1]
+                )
+
+        def stage_g(j, s):
+            if s == 0:
+                acts[j] = work3.tile([P, GT * 4 * HID], F32, name="acts")
+            g = psum.tile([P, 4 * HID], F32, name="g", tag="bank")
+            for n in range(4):
+                nc.tensor.matmul(
+                    out=g[:, n * HID : (n + 1) * HID],
+                    lhsT=a_sb[j][:, n * GW + s * P : n * GW + (s + 1) * P],
+                    rhs=ident_f[:],
+                    is_transpose=True,
+                    start=(n == 0),
+                    stop=False,
+                )
+            nc.tensor.matmul(out=g[:], lhsT=h_t_sb[j][:, s * P : (s + 1) * P], rhs=u_t[:], start=False, stop=True)
+            base = s * 4 * HID
+            nc.scalar.activation(out=acts[j][:, base : base + 4 * HID], in_=g[:], func=ACT.Sigmoid)
 
         def by_tile(ap, tiles):
             return ap.rearrange("p (t h) -> p t h", t=tiles)
@@ -211,23 +233,36 @@ def tile_lstmcell_t_kernel(
         def gate(j, n, s0, s1):
             return acts[j][:].rearrange("p (t n h) -> p t n h", t=GT, n=4)[:, s0:s1, n, :]
 
-        def stage_prod(j, eng, s0, s1):
+        def stage_fc(j, eng, s0, s1):
             tiles = s1 - s0
             key = (j, s0)
             fc[key] = work2.tile([P, tiles * HID], F32, name="fc")
-            ic[key] = work2.tile([P, tiles * HID], F32, name="ic")
             eng.tensor_tensor(
                 out=by_tile(fc[key][:], tiles),
                 in0=gate(j, 1, s0, s1),
                 in1=by_tile(c_of[j][:, s0 * HID : s1 * HID], tiles),
                 op=ALU.mult,
             )
-            eng.tensor_tensor(out=by_tile(ic[key][:], tiles), in0=gate(j, 0, s0, s1), in1=gate(j, 3, s0, s1), op=ALU.mult)
+
+        def stage_ic(j, s0, s1):
+            tiles = s1 - s0
+            key = (j, s0)
+            ic[key] = work2.tile([P, tiles * HID], F32, name="ic")
+            nc.vector.scalar_tensor_tensor(
+                out=by_tile(ic[key][:], tiles),
+                in0=gate(j, 3, s0, s1),
+                scalar=-0.5,
+                in1=gate(j, 0, s0, s1),
+                op0=ALU.add,
+                op1=ALU.mult,
+            )
 
         def stage_add(j, s0, s1):
             key = (j, s0)
             cell[key] = work4.tile([P, (s1 - s0) * HID], F32, name="cell")
-            nc.vector.tensor_tensor(out=cell[key][:], in0=fc[key][:], in1=ic[key][:], op=ALU.add)
+            nc.vector.scalar_tensor_tensor(
+                out=cell[key][:], in0=ic[key][:], scalar=2.0, in1=fc[key][:], op0=ALU.mult, op1=ALU.add
+            )
             nc.sync.dma_start(out=cell_rows[:, j * GW + s0 * HID : j * GW + s1 * HID], in_=cell[key][:])
 
         def stage_tanh(j, s0, s1):
@@ -235,86 +270,114 @@ def tile_lstmcell_t_kernel(
             tanh_c[key] = work2.tile([P, (s1 - s0) * HID], F32, name="tanh_c")
             nc.scalar.activation(out=tanh_c[key][:], in_=cell[key][:], func=ACT.Tanh)
 
-        def stage_h(j, s0, s1):
+        def stage_h(j, eng, s0, s1):
             tiles = s1 - s0
             nh = work4.tile([P, tiles * HID], F32, name="nh")
-            nc.vector.tensor_tensor(
+            eng.tensor_tensor(
                 out=by_tile(nh[:], tiles), in0=gate(j, 2, s0, s1), in1=by_tile(tanh_c[(j, s0)][:], tiles), op=ALU.mult
             )
             nc.sync.dma_start(out=nh_rows[:, j * GW + s0 * HID : j * GW + s1 * HID], in_=nh[:])
 
-        on_s = [nc.scalar.copy, nc.scalar.copy]
-
         w_grouped = const.tile([P, 4 * P * 4], BF16, name="w_grouped", align_bytes=64)
-        transpose_words(w_sb, w_grouped, [nc.vector.tensor_copy, nc.vector.tensor_copy])
+        transpose_half(w_sb, w_grouped, 0, on_vector, None)
+        transpose_half(w_sb, w_grouped, 1, on_vector, None)
         w_codes = const.tile([P, 4 * P], U32, name="w_codes", align_bytes=64)
         w_scales = const.tile([P, 4 * P], U8, name="w_scales", align_bytes=64)
         nc.vector.quantize_mx(out=w_codes[:].bitcast(FP8X4), scales=w_scales[:], in_=w_grouped[:])
 
-        stage_tx(0, [nc.scalar.copy, nc.vector.tensor_copy])
+        stage_tx(0, 0, on_scalar)
+        stage_tx(0, 1, on_vector)
         stage_th(0)
+        stage_hcopy(0, on_vector)
 
         ut = psum.tile([P, 4 * HID], BF16, name="ut", tag="bank")
         for n in range(4):
             nc.tensor.transpose(ut[:, n * HID : (n + 1) * HID], u_sb[:, n * HID : (n + 1) * HID], ident_b[:])
         u_t = const.tile([P, 4 * HID], BF16, name="u_t")
-        nc.vector.tensor_copy(out=u_t[:], in_=ut[:])
+        nc.vector.tensor_copy(out=u_t[:, 0 : 3 * HID], in_=ut[:, 0 : 3 * HID])
+        nc.vector.tensor_scalar_mul(out=u_t[:, 3 * HID : 4 * HID], in0=ut[:, 3 * HID : 4 * HID], scalar1=2.0)
         bt = psum.tile([P, P], BF16, name="bt", tag="bank")
         nc.tensor.transpose(bt[:], b_rows[:], ident_b[:])
         bias_col = const.tile([P, 4], F32, name="bias_col")
         nc.vector.tensor_copy(out=bias_col[:], in_=bt[:, 0:4])
-
         stage_q(0)
-        stage_tx(1, on_s)
+
+        stage_tx(1, 0, on_scalar)
+        stage_tx(1, 1, on_scalar)
         stage_th(1)
-        stage_mx(0, [1, 3])
+        stage_hcopy(1, on_vector)
+        stage_mx(0)
+        for n in range(4):
+            stage_mxcopy(0, n, n in (0, 1))
         stage_q(1)
-        stage_tx(2, on_s)
+        stage_tx(2, 0, on_scalar)
+        stage_tx(2, 1, on_scalar)
         stage_th(2)
-        stage_mx(1, [])
+        stage_hcopy(2, on_vector)
+        stage_mx(1)
+        for n in range(4):
+            stage_mxcopy(1, n, False)
         stage_q(2)
+
         for i in range(NG - 2):
             if i + 3 < NG:
-                stage_tx(i + 3, on_s)
+                stage_tx(i + 3, 0, on_scalar)
+                stage_tx(i + 3, 1, on_scalar)
                 stage_th(i + 3)
+                stage_hcopy(i + 3, on_vector)
             if i >= 1:
-                stage_prod(i - 1, nc.gpsimd, 0, GT)
+                stage_fc(i - 1, nc.gpsimd, 0, GT)
+            if i >= 2:
+                stage_h(i - 2, nc.gpsimd, 0, GT)
+            if i >= 1:
+                stage_ic(i - 1, 0, GT)
             if i + 3 < NG:
                 stage_q(i + 3)
+            if i + 4 < NG:
+                stage_part(i + 4, 1, on_vector)
             if i >= 1:
                 stage_add(i - 1, 0, GT)
-            if i >= 2:
-                stage_h(i - 2, 0, GT)
-            stage_g(i, 0, GT)
+            for s in range(GT):
+                stage_g(i, s)
             if i >= 1:
                 stage_tanh(i - 1, 0, GT)
             if i + 2 < NG:
-                stage_mx(i + 2, [])
+                stage_mx(i + 2)
+                for n in range(4):
+                    stage_mxcopy(i + 2, n, False)
 
         ga = NG - 3
         gb = NG - 2
         gc = NG - 1
-        stage_prod(ga, nc.gpsimd, 0, GT)
-        stage_g(gb, 0, 4)
-        stage_h(ga - 1, 0, GT)
-        stage_prod(gb, nc.vector, 0, 2)
-        stage_add(gb, 0, 2)
+        stage_fc(ga, nc.gpsimd, 0, GT)
+        stage_h(ga - 1, nc.gpsimd, 0, GT)
+        for s in range(4):
+            stage_g(gb, s)
+        stage_ic(ga, 0, GT)
+        stage_fc(gb, nc.vector, 0, 2)
         stage_add(ga, 0, GT)
-        stage_g(gc, 0, 2)
+        stage_ic(gb, 0, 2)
+        stage_g(gc, 0)
+        stage_g(gc, 1)
         stage_tanh(ga, 0, GT)
-        stage_prod(gb, nc.vector, 2, 4)
+        stage_fc(gb, nc.vector, 2, 4)
+        stage_add(gb, 0, 2)
+        stage_ic(gb, 2, 4)
+        stage_h(ga, nc.vector, 0, GT)
         stage_add(gb, 2, 4)
         stage_tanh(gb, 0, 2)
-        stage_h(ga, 0, GT)
-        stage_g(gc, 2, 4)
+        stage_g(gc, 2)
+        stage_g(gc, 3)
         stage_tanh(gb, 2, 4)
-        stage_h(gb, 0, 2)
-        stage_prod(gc, nc.vector, 0, 2)
+        stage_fc(gc, nc.vector, 0, 2)
+        stage_ic(gc, 0, 2)
+        stage_h(gb, nc.vector, 0, 2)
         stage_add(gc, 0, 2)
-        stage_h(gb, 2, 4)
+        stage_h(gb, nc.vector, 2, 4)
         stage_tanh(gc, 0, 2)
-        stage_prod(gc, nc.vector, 2, 4)
+        stage_fc(gc, nc.vector, 2, 4)
+        stage_ic(gc, 2, 4)
+        stage_h(gc, nc.vector, 0, 2)
         stage_add(gc, 2, 4)
-        stage_h(gc, 0, 2)
         stage_tanh(gc, 2, 4)
-        stage_h(gc, 2, 4)
+        stage_h(gc, nc.vector, 2, 4)

@@ -308,70 +308,60 @@ def tile_lstmcell_t_kernel(
         stage_hcopy(1, on_vector)
         stage_mx(0)
         for n in range(4):
-            stage_mxcopy(0, n, n in (0, 1))
+            stage_mxcopy(0, n, n in (0, 2))
         stage_q(1)
-        stage_tx(2, 0, on_scalar)
-        stage_tx(2, 1, on_scalar)
-        stage_th(2)
-        stage_hcopy(2, on_vector)
-        stage_mx(1)
-        for n in range(4):
-            stage_mxcopy(1, n, False)
-        stage_q(2)
 
         for i in range(NG - 2):
-            if i + 3 < NG:
-                stage_tx(i + 3, 0, on_scalar)
-                stage_tx(i + 3, 1, on_scalar)
-                stage_th(i + 3)
-                stage_hcopy(i + 3, on_vector)
+            stage_tx(i + 2, 0, on_scalar)
+            stage_tx(i + 2, 1, on_scalar)
+            stage_th(i + 2)
+            stage_hcopy(i + 2, on_vector)
             if i >= 1:
                 stage_fc(i - 1, nc.gpsimd, 0, GT)
-            if i >= 2:
-                stage_h(i - 2, nc.gpsimd, 0, GT)
-            if i >= 1:
                 stage_ic(i - 1, 0, GT)
-            if i + 3 < NG:
-                stage_q(i + 3)
-            if i + 4 < NG:
-                stage_part(i + 4, 1, on_vector)
+            stage_q(i + 2)
             if i >= 1:
                 stage_add(i - 1, 0, GT)
+            if i >= 2:
+                stage_h(i - 2, nc.vector, 0, GT)
             for s in range(GT):
                 stage_g(i, s)
+
+            stage_mx(i + 1)
+            for n in range(4):
+                stage_mxcopy(i + 1, n, n in (1,))
             if i >= 1:
                 stage_tanh(i - 1, 0, GT)
-            if i + 2 < NG:
-                stage_mx(i + 2)
-                for n in range(4):
-                    stage_mxcopy(i + 2, n, False)
 
         ga = NG - 3
         gb = NG - 2
         gc = NG - 1
+        stage_mx(gc)
+        for n in range(4):
+            stage_mxcopy(gc, n, n in (0, 2))
         stage_fc(ga, nc.gpsimd, 0, GT)
-        stage_h(ga - 1, nc.gpsimd, 0, GT)
+        stage_ic(ga, 0, GT)
+        stage_h(ga - 1, nc.vector, 0, GT)
+        stage_add(ga, 0, GT)
         for s in range(4):
             stage_g(gb, s)
-        stage_ic(ga, 0, GT)
+        stage_tanh(ga, 0, GT)
         stage_fc(gb, nc.vector, 0, 2)
-        stage_add(ga, 0, GT)
         stage_ic(gb, 0, 2)
+        stage_h(ga, nc.vector, 0, GT)
+        stage_add(gb, 0, 2)
+        stage_fc(gb, nc.vector, 2, 4)
+        stage_ic(gb, 2, 4)
         stage_g(gc, 0)
         stage_g(gc, 1)
-        stage_tanh(ga, 0, GT)
-        stage_fc(gb, nc.vector, 2, 4)
-        stage_add(gb, 0, 2)
-        stage_ic(gb, 2, 4)
-        stage_h(ga, nc.vector, 0, GT)
-        stage_add(gb, 2, 4)
         stage_tanh(gb, 0, 2)
+        stage_add(gb, 2, 4)
+        stage_h(gb, nc.vector, 0, 2)
+        stage_fc(gc, nc.vector, 0, 2)
+        stage_ic(gc, 0, 2)
         stage_g(gc, 2)
         stage_g(gc, 3)
         stage_tanh(gb, 2, 4)
-        stage_fc(gc, nc.vector, 0, 2)
-        stage_ic(gc, 0, 2)
-        stage_h(gb, nc.vector, 0, 2)
         stage_add(gc, 0, 2)
         stage_h(gb, nc.vector, 2, 4)
         stage_tanh(gc, 0, 2)

@@ -287,9 +287,14 @@ def tile_lstmcell_t_kernel(
 
         stage_tx(0, 0, on_scalar)
         stage_tx(0, 1, on_vector)
+        stage_q(0)
         stage_th(0)
         stage_hcopy(0, on_vector)
 
+        stage_tx(1, 0, on_scalar)
+        stage_tx(1, 1, on_scalar)
+        stage_th(1)
+        stage_hcopy(1, on_vector)
         ut = psum.tile([P, 4 * HID], BF16, name="ut", tag="bank")
         for n in range(4):
             nc.tensor.transpose(ut[:, n * HID : (n + 1) * HID], u_sb[:, n * HID : (n + 1) * HID], ident_b[:])
@@ -300,12 +305,6 @@ def tile_lstmcell_t_kernel(
         nc.tensor.transpose(bt[:], b_rows[:], ident_b[:])
         bias_col = const.tile([P, 4], F32, name="bias_col")
         nc.vector.tensor_copy(out=bias_col[:], in_=bt[:, 0:4])
-        stage_q(0)
-
-        stage_tx(1, 0, on_scalar)
-        stage_tx(1, 1, on_scalar)
-        stage_th(1)
-        stage_hcopy(1, on_vector)
         stage_mx(0)
         for n in range(4):
             stage_mxcopy(0, n, n in (0, 2))
@@ -337,15 +336,18 @@ def tile_lstmcell_t_kernel(
         gb = NG - 2
         gc = NG - 1
         stage_mx(gc)
-        for n in range(4):
-            stage_mxcopy(gc, n, n in (0, 2))
         stage_fc(ga, nc.gpsimd, 0, GT)
         stage_ic(ga, 0, GT)
-        stage_h(ga - 1, nc.vector, 0, GT)
         stage_add(ga, 0, GT)
+        for n in range(4):
+            stage_mxcopy(gc, n, n in (0, 2))
+        stage_h(ga - 1, nc.vector, 0, GT)
         for s in range(4):
+            if s == 2:
+                stage_tanh(ga, 0, GT)
             stage_g(gb, s)
-        stage_tanh(ga, 0, GT)
+        if 2 == 4:
+            stage_tanh(ga, 0, GT)
         stage_fc(gb, nc.vector, 0, 2)
         stage_ic(gb, 0, 2)
         stage_h(ga, nc.vector, 0, GT)

@@ -318,11 +318,11 @@ def tile_lstmcell_t_kernel(
             if i >= 1:
                 stage_fc(i - 1, nc.gpsimd, 0, GT)
                 stage_ic(i - 1, 0, GT)
-            stage_q(i + 2)
-            if i >= 1:
-                stage_add(i - 1, 0, GT)
             if i >= 2:
                 stage_h(i - 2, nc.vector, 0, GT)
+            if i >= 1:
+                stage_add(i - 1, 0, GT)
+            stage_q(i + 2)
             for s in range(GT):
                 stage_g(i, s)
 

from contextlib import ExitStack

import concourse.mybir as mybir
from concourse.masks import make_identity

F32 = mybir.dt.float32
BF16 = mybir.dt.bfloat16
U32 = mybir.dt.uint32
U8 = mybir.dt.uint8
FP8X4 = mybir.dt.float8_e4m3fn_x4
ACT = mybir.ActivationFunctionType
ALU = mybir.AluOpType

P = 128
BATCH = 8192
IN_F = 512
HID = 128
NT = BATCH // P
GT = 4
NG = NT // GT
GW = GT * P
HC_SIZES = [2, 2, 4, 4, 4]

FLOPS = 2 * BATCH * (IN_F + HID) * 4 * HID


def tile_lstmcell_t_kernel(
    tc, incoming, old_h, old_c, w_i, b_i, u_i, w_o, b_o, u_o, w_f, b_f, u_f, w_c, b_c, u_c, out_0, out_1
):
    nc = tc.nc
    gate_w = [w_i, w_f, w_o, w_c]
    gate_u = [u_i, u_f, u_o, u_c]
    gate_b = [b_i, b_f, b_o, b_c]

    x_rows = incoming.rearrange("(p t) k -> p (t k)", t=NT)
    h_rows = old_h.rearrange("(p t) k -> p (t k)", t=NT)
    c_rows = old_c.rearrange("(p t) k -> p (t k)", t=NT)
    nh_rows = out_0.rearrange("(p t) k -> p (t k)", t=NT)
    cell_rows = out_1.rearrange("(p t) k -> p (t k)", t=NT)

    with ExitStack() as ctx:
        const = ctx.enter_context(tc.tile_pool(name="const", bufs=1))
        resident = ctx.enter_context(tc.tile_pool(name="resident", bufs=1))
        work2 = ctx.enter_context(tc.tile_pool(name="work2", bufs=2))
        work3 = ctx.enter_context(tc.tile_pool(name="work3", bufs=3))
        work4 = ctx.enter_context(tc.tile_pool(name="work4", bufs=4))
        psum = ctx.enter_context(tc.psum_pool(name="psum", bufs=8))
        ctx.enter_context(tc.manual_schedule())

        ident_f = const.tile([P, P], F32, name="ident_f")
        make_identity(nc, ident_f[:])
        ident_b = const.tile([P, P], BF16, name="ident_b")
        make_identity(nc, ident_b[:])

        warm = const.tile([P, 1], F32, name="warm")
        nc.vector.memset(warm[:], 0.0)
        warm_out = const.tile([P, 1], F32, name="warm_out")
        nc.scalar.activation(out=warm_out[:], in_=warm[:], func=ACT.Sigmoid)

        x_sb = {}
        h_of = {}
        c_of = {}

        def load_x(j):
            x_sb[j] = resident.tile([P, GT * IN_F], BF16, name="x%d" % j)
            nc.sync.dma_start(out=x_sb[j][:], in_=x_rows[:, j * GT * IN_F : (j + 1) * GT * IN_F])

        def load_hc(m, rows, table, letter):
            first = sum(HC_SIZES[:m])
            t = resident.tile([P, HC_SIZES[m] * GW], BF16, name="%s%d" % (letter, m))
            nc.sync.dma_start(out=t[:], in_=rows[:, first * GW : (first + HC_SIZES[m]) * GW])
            for r in range(HC_SIZES[m]):
                table[first + r] = t[:, r * GW : (r + 1) * GW]

        def load_h(m):
            load_hc(m, h_rows, h_of, "h")

        def load_c(m):
            load_hc(m, c_rows, c_of, "c")

        w_sb = const.tile([P, 4 * IN_F], BF16, name="w_sb")
        for n in range(4):
            nc.sync.dma_start(out=w_sb[:, n * IN_F : (n + 1) * IN_F], in_=gate_w[n])
        load_x(0)
        load_h(0)
        u_sb = const.tile([P, 4 * HID], BF16, name="u_sb")
        for n in range(4):
            nc.scalar.dma_start(out=u_sb[:, n * HID : (n + 1) * HID], in_=gate_u[n])
        b_rows = const.tile([P, P], BF16, name="b_rows")
        nc.vector.memset(b_rows[:], 0.0)
        for n in range(4):
            nc.scalar.dma_start(out=b_rows[n : n + 1, :], in_=gate_b[n].rearrange("(o h) -> o h", o=1))
        load_x(1)
        load_x(2)
        load_c(0)
        load_h(1)
        load_x(3)
        load_c(1)
        load_x(4)
        load_h(2)
        load_x(5)
        load_c(2)
        load_x(6)
        load_x(7)
        load_x(8)
        load_h(3)
        load_c(3)
        load_x(9)
        load_x(10)
        load_x(11)
        load_x(12)
        load_h(4)
        load_c(4)
        load_x(13)
        load_x(14)
        load_x(15)

        parted = {}
        grouped = {}
        codes = {}
        scales = {}
        h_bank = {}
        h_t_sb = {}
        a_sb = {}
        mx_bank = {}
        acts = {}
        fc = {}
        ic = {}
        cell = {}
        tanh_c = {}
        on_scalar = nc.scalar.copy
        on_vector = nc.vector.tensor_copy
        on_gpsimd = nc.gpsimd.tensor_copy

        def half_words(src, half):
            return src[:].bitcast(F32)[:, half * 512 : (half + 1) * 512]

        def stage_part(j, half, copy):
            parted[(j, half)] = work3.tile([P, 512], F32, name="parted%d" % half)
            copy(
                out=parted[(j, half)][:].rearrange("q (u w) -> q u w", u=2),
                in_=half_words(x_sb[j], half).rearrange("q (w u) -> q u w", u=2),
            )

        def transpose_half(src, dst, half, copy, part):
            out_words = dst[:].bitcast(F32).rearrange("q (s c u) -> q s c u", s=4, u=2)
            bank = psum.tile([P, 512], F32, name="bank", tag="bank")
            for s in range(2):
                for u in range(2):
                    if part is None:
                        ap = half_words(src, half)[:, s * 256 + u : (s + 1) * 256 : 2]
                    else:
                        ap = part[:, u * 256 + s * P : u * 256 + (s + 1) * P]
                    nc.tensor.transpose(bank[:, (2 * s + u) * P : (2 * s + u + 1) * P], ap, ident_f[:])
            copy(
                out=out_words[:, 2 * half : 2 * half + 2],
                in_=bank[:].rearrange("q (s u c) -> q s c u", s=2, u=2),
            )

        def stage_tx(j, half, copy):
            if half == 0:
                grouped[j] = work2.tile([P, GW * 4], BF16, name="grouped", align_bytes=64)
            part = parted.get((j, half))
            transpose_half(x_sb[j], grouped[j], half, copy, None if part is None else part[:])

        def stage_th(j):
            h_bank[j] = psum.tile([P, GW], BF16, name="ht", tag="bank")
            for s in range(GT):
                nc.tensor.transpose(h_bank[j][:, s * P : (s + 1) * P], h_of[j][:, s * P : (s + 1) * P], ident_b[:])

        def stage_hcopy(j, copy):
            h_t_sb[j] = work4.tile([P, GW], BF16, name="h_t_sb")
            copy(out=h_t_sb[j][:], in_=h_bank[j][:])

        def stage_q(j):
            codes[j] = work3.tile([P, GW], U32, name="codes", align_bytes=64)
            scales[j] = work3.tile([P, GW], U8, name="scales", align_bytes=64)
            nc.vector.quantize_mx(out=codes[j][:].bitcast(FP8X4), scales=scales[j][:], in_=grouped[j][:])

        def stage_mx(j):
            a_sb[j] = work3.tile([P, 4 * GW], F32, name="a_sb")
            for n in range(4):
                mx_bank[(j, n)] = psum.tile([P, GW], F32, name="mx", tag="bank")
                nc.tensor.matmul_mx(
                    out=mx_bank[(j, n)][:],
                    lhsT=w_codes[:, n * P : (n + 1) * P].bitcast(FP8X4),
                    lhsT_scale=w_scales[:, n * P : (n + 1) * P],
                    rhs=codes[j][:].bitcast(FP8X4),
                    rhs_scale=scales[j][:],
                    start=True,
                    stop=True,
                )

        def stage_mxcopy(j, n, scalar):
            if scalar:
                nc.scalar.activation(
                    out=a_sb[j][:, n * GW : (n + 1) * GW], in_=mx_bank[(j, n)][:], func=ACT.Identity, bias=bias_col[:, n : n + 1]
                )
            elif n == 3:
                nc.vector.tensor_scalar(
                    out=a_sb[j][:, n * GW : (n + 1) * GW],
                    in0=mx_bank[(j, n)][:],
                    scalar1=bias_col[:, n : n + 1],
                    scalar2=2.0,
                    op0=ALU.add,
                    op1=ALU.mult,
                )
            else:
                nc.vector.tensor_scalar_add(
                    out=a_sb[j][:, n * GW : (n + 1) * GW], in0=mx_bank[(j, n)][:], scalar1=bias_col[:, n : n + 1]
                )

        def stage_g(j, s):
            if s == 0:
                acts[j] = work3.tile([P, GT * 4 * HID], F32, name="acts")
            g = psum.tile([P, 4 * HID], F32, name="g", tag="bank")
            for n in range(4):
                nc.tensor.matmul(
                    out=g[:, n * HID : (n + 1) * HID],
                    lhsT=a_sb[j][:, n * GW + s * P : n * GW + (s + 1) * P],
                    rhs=ident_f[:],
                    is_transpose=True,
                    start=(n == 0),
                    stop=False,
                )
            nc.tensor.matmul(out=g[:], lhsT=h_t_sb[j][:, s * P : (s + 1) * P], rhs=u_t[:], start=False, stop=True)
            base = s * 4 * HID
            nc.scalar.activation(out=acts[j][:, base : base + 4 * HID], in_=g[:], func=ACT.Sigmoid)

        def by_tile(ap, tiles):
            return ap.rearrange("p (t h) -> p t h", t=tiles)

        def gate(j, n, s0, s1):
            return acts[j][:].rearrange("p (t n h) -> p t n h", t=GT, n=4)[:, s0:s1, n, :]

        def stage_fc(j, eng, s0, s1):
            tiles = s1 - s0
            key = (j, s0)
            fc[key] = work2.tile([P, tiles * HID], F32, name="fc")
            eng.tensor_tensor(
                out=by_tile(fc[key][:], tiles),
                in0=gate(j, 1, s0, s1),
                in1=by_tile(c_of[j][:, s0 * HID : s1 * HID], tiles),
                op=ALU.mult,
            )

        def stage_ic(j, s0, s1):
            tiles = s1 - s0
            key = (j, s0)
            ic[key] = work2.tile([P, tiles * HID], F32, name="ic")
            nc.vector.scalar_tensor_tensor(
                out=by_tile(ic[key][:], tiles),
                in0=gate(j, 3, s0, s1),
                scalar=-0.5,
                in1=gate(j, 0, s0, s1),
                op0=ALU.add,
                op1=ALU.mult,
            )

        def stage_add(j, s0, s1):
            key = (j, s0)
            cell[key] = work4.tile([P, (s1 - s0) * HID], F32, name="cell")
            nc.vector.scalar_tensor_tensor(
                out=cell[key][:], in0=ic[key][:], scalar=2.0, in1=fc[key][:], op0=ALU.mult, op1=ALU.add
            )
            nc.sync.dma_start(out=cell_rows[:, j * GW + s0 * HID : j * GW + s1 * HID], in_=cell[key][:])

        def stage_tanh(j, s0, s1):
            key = (j, s0)
            tanh_c[key] = work2.tile([P, (s1 - s0) * HID], F32, name="tanh_c")
            nc.scalar.activation(out=tanh_c[key][:], in_=cell[key][:], func=ACT.Tanh)

        def stage_h(j, eng, s0, s1):
            tiles = s1 - s0
            nh = work4.tile([P, tiles * HID], F32, name="nh")
            eng.tensor_tensor(
                out=by_tile(nh[:], tiles), in0=gate(j, 2, s0, s1), in1=by_tile(tanh_c[(j, s0)][:], tiles), op=ALU.mult
            )
            nc.sync.dma_start(out=nh_rows[:, j * GW + s0 * HID : j * GW + s1 * HID], in_=nh[:])

        w_grouped = const.tile([P, 4 * P * 4], BF16, name="w_grouped", align_bytes=64)
        transpose_half(w_sb, w_grouped, 0, on_vector, None)
        transpose_half(w_sb, w_grouped, 1, on_vector, None)
        w_codes = const.tile([P, 4 * P], U32, name="w_codes", align_bytes=64)
        w_scales = const.tile([P, 4 * P], U8, name="w_scales", align_bytes=64)
        nc.vector.quantize_mx(out=w_codes[:].bitcast(FP8X4), scales=w_scales[:], in_=w_grouped[:])

        stage_tx(0, 0, on_scalar)
        stage_tx(0, 1, on_vector)
        stage_q(0)
        stage_th(0)
        stage_hcopy(0, on_vector)

        stage_tx(1, 0, on_scalar)
        stage_tx(1, 1, on_scalar)
        stage_th(1)
        stage_hcopy(1, on_vector)
        ut = psum.tile([P, 4 * HID], BF16, name="ut", tag="bank")
        for n in range(4):
            nc.tensor.transpose(ut[:, n * HID : (n + 1) * HID], u_sb[:, n * HID : (n + 1) * HID], ident_b[:])
        u_t = const.tile([P, 4 * HID], BF16, name="u_t")
        nc.vector.tensor_copy(out=u_t[:, 0 : 3 * HID], in_=ut[:, 0 : 3 * HID])
        nc.vector.tensor_scalar_mul(out=u_t[:, 3 * HID : 4 * HID], in0=ut[:, 3 * HID : 4 * HID], scalar1=2.0)
        bt = psum.tile([P, P], BF16, name="bt", tag="bank")
        nc.tensor.transpose(bt[:], b_rows[:], ident_b[:])
        bias_col = const.tile([P, 4], F32, name="bias_col")
        nc.vector.tensor_copy(out=bias_col[:], in_=bt[:, 0:4])
        stage_mx(0)
        for n in range(4):
            stage_mxcopy(0, n, n in (0, 2))
        stage_q(1)

        for i in range(NG - 2):
            stage_tx(i + 2, 0, on_scalar)
            stage_tx(i + 2, 1, on_scalar)
            stage_th(i + 2)
            stage_hcopy(i + 2, on_vector)
            if i >= 1:
                stage_fc(i - 1, nc.gpsimd, 0, GT)
                stage_ic(i - 1, 0, GT)
            if i >= 2:
                stage_h(i - 2, nc.vector, 0, GT)
            if i >= 1:
                stage_add(i - 1, 0, GT)
            stage_q(i + 2)
            for s in range(GT):
                stage_g(i, s)

            stage_mx(i + 1)
            for n in range(4):
                stage_mxcopy(i + 1, n, n in (1,))
            if i >= 1:
                stage_tanh(i - 1, 0, GT)

        ga = NG - 3
        gb = NG - 2
        gc = NG - 1
        stage_mx(gc)
        stage_fc(ga, nc.gpsimd, 0, GT)
        stage_ic(ga, 0, GT)
        stage_add(ga, 0, GT)
        for n in range(4):
            stage_mxcopy(gc, n, n in (0, 2))
        stage_h(ga - 1, nc.vector, 0, GT)
        for s in range(4):
            if s == 2:
                stage_tanh(ga, 0, GT)
            stage_g(gb, s)
        if 2 == 4:
            stage_tanh(ga, 0, GT)
        stage_fc(gb, nc.vector, 0, 2)
        stage_ic(gb, 0, 2)
        stage_h(ga, nc.vector, 0, GT)
        stage_add(gb, 0, 2)
        stage_fc(gb, nc.vector, 2, 4)
        stage_ic(gb, 2, 4)
        stage_g(gc, 0)
        stage_g(gc, 1)
        stage_tanh(gb, 0, 2)
        stage_add(gb, 2, 4)
        stage_h(gb, nc.vector, 0, 2)
        stage_fc(gc, nc.vector, 0, 2)
        stage_ic(gc, 0, 2)
        stage_g(gc, 2)
        stage_g(gc, 3)
        stage_tanh(gb, 2, 4)
        stage_add(gc, 0, 2)
        stage_h(gb, nc.vector, 2, 4)
        stage_tanh(gc, 0, 2)
        stage_fc(gc, nc.vector, 2, 4)
        stage_ic(gc, 2, 4)
        stage_h(gc, nc.vector, 0, 2)
        stage_add(gc, 2, 4)
        stage_tanh(gc, 2, 4)
        stage_h(gc, nc.vector, 2, 4)
